import numpy as np
import ml_dtypes


def mxq(x, axis, fmt="e4m3"):
    dtype, down = {"e4m3": (ml_dtypes.float8_e4m3fn, 7), "e5m2": (ml_dtypes.float8_e5m2, 14)}[fmt]
    v = np.moveaxis(np.asarray(x, np.float32).astype(ml_dtypes.bfloat16).astype(np.float64), axis, -1)
    blocks = v.reshape(v.shape[:-1] + (-1, 32))
    amax = np.abs(blocks).max(-1, keepdims=True)
    byte = np.maximum(np.where(amax > 0, np.frexp(amax)[1] - 1 + 127, 0) - down, 1)
    scale = np.exp2(byte - 127.0)
    codes = (blocks / scale).astype(np.float32).astype(dtype).astype(np.float64)
    return np.moveaxis((codes * scale).reshape(v.shape), -1, axis)


WIDE = False


def mx_kscale(k):
    if not WIDE:
        return np.ones(k)
    levels = np.array([10, -10, 5, -5, 0])
    a = np.random.permutation(np.resize(levels, k // 512 * 4)).reshape(k // 512, 4)
    idx = np.arange(k)
    return np.exp2(a[idx // 512, idx % 128 // 32])


BF16 = ml_dtypes.bfloat16


def bf(x):
    return np.asarray(x, np.float32).astype(BF16)


def f64(x):
    return np.asarray(x).astype(np.float64)


E2M1 = np.array([0.0, 0.5, 1.0, 1.5, 2.0, 3.0, 4.0, 6.0, -0.0, -0.5, -1.0, -1.5, -2.0, -3.0, -4.0, -6.0])


def pack_weight(w, fmt):
    k, n = w.shape
    w = f64(bf(w)).reshape(k // 32, 32, n)
    amax = np.abs(w).max(1)
    if fmt == "e4m3":
        byte = np.frexp(amax)[1] - 1 + 127 - 7
    else:
        mant, ex = np.frexp(amax / 6.0)
        byte = np.where(mant > 0.5, ex, ex - 1) + 127
    byte = np.clip(np.where(amax > 0, byte, 1), 1, 254)
    scaled = (w * np.exp2(127.0 - byte)[:, None, :]).reshape(k, n).astype(np.float32)
    by_word = np.ascontiguousarray(scaled.reshape(k // 512, 128, 4, n).transpose(0, 1, 3, 2))
    if fmt == "e4m3":
        words = by_word.astype(ml_dtypes.float8_e4m3fn).view(np.uint8)
    else:
        c = by_word.astype(ml_dtypes.float4_e2m1fn).view(np.uint8) & 0xF
        words = c[..., 0::2] | (c[..., 1::2] << 4)
    return np.ascontiguousarray(words), np.ascontiguousarray(byte.astype(np.uint8).reshape(k // 512, 16, n))


def unpack_weight(words, scales, fmt):
    g, p, n, _ = words.shape
    if fmt == "e4m3":
        vals = np.ascontiguousarray(words).view(ml_dtypes.float8_e4m3fn).astype(np.float64)
    else:
        nib = np.empty((g, p, n, 4), np.uint8)
        nib[..., 0::2] = words & 0xF
        nib[..., 1::2] = words >> 4
        vals = E2M1[nib]
    vals = vals * np.repeat(np.exp2(scales.astype(np.float64) - 127.0), 8, axis=1)[..., None]
    return vals.transpose(0, 1, 3, 2).reshape(g * 512, n)


B, D, H, G = 128, 512, 1024, 7
K = D + H
FMT = "e4m3"


def sigmoid(v):
    return 1.0 / (1.0 + np.exp(-v))


def softplus(v):
    return np.log(1.0 + np.exp(v))


def setup_inputs():
    s = mx_kscale(K)
    x = bf(np.random.standard_normal((B, D)) * s[:D])
    h_t = bf(np.random.standard_normal((B, H)) * s[D:])
    c_t = bf(np.random.standard_normal((B, H)))
    c_target = bf(np.random.standard_normal((B, H)))
    W1 = np.random.standard_normal((G, H, K)) / np.sqrt(K) / s
    b1 = bf(np.random.standard_normal((G, H)) * 0.2)
    W2 = np.random.standard_normal((G, H, H)) * 2.0 / np.sqrt(H)
    b2 = bf(np.random.standard_normal((G, H)) * 0.2)
    W1_words, W1_scales = pack_weight(W1.swapaxes(1, 2).reshape(-1, H), FMT)
    W2_words, W2_scales = pack_weight(W2.reshape(-1, H), FMT)
    return {"x": x,
            "h_t": h_t,
            "c_t": c_t,
            "c_target": c_target,
            "W1_words": W1_words,
            "W1_scales": W1_scales,
            "b1": b1,
            "W2_words": W2_words,
            "W2_scales": W2_scales,
            "b2": b2}


def reference(x, h_t, c_t, c_target, W1_words, W1_scales, b1, W2_words, W2_scales, b2):
    v = np.concatenate([f64(x), f64(h_t)], axis=1)
    h1 = np.tanh((mxq(v, 1, "e4m3") @ unpack_weight(W1_words, W1_scales, FMT).reshape(G, K, H)) + f64(b1)[:, None, :])
    g = (mxq(h1, 2, "e4m3") @ unpack_weight(W2_words, W2_scales, FMT).reshape(G, H, H)) + f64(b2)[:, None, :]
    inpt = sigmoid(g[0])
    forget = sigmoid(g[1])
    input_target = sigmoid(g[2])
    forget_target = sigmoid(g[3])
    output = sigmoid(g[4])
    z_i = np.tanh(g[5])
    decay = softplus(g[6])
    c_i = forget * f64(c_t) + inpt * z_i
    c_target_new = forget_target * f64(c_target) + input_target * z_i
    return (c_i, c_target_new, output, decay)

@@ -1,0 +1,320 @@
+from contextlib import ExitStack
+
+import concourse.mybir as mybir
+from concourse.masks import make_identity
+
+F32 = mybir.dt.float32
+BF16 = mybir.dt.bfloat16
+I32 = mybir.dt.int32
+U32 = mybir.dt.uint32
+U8 = mybir.dt.uint8
+FP8X4 = mybir.dt.float8_e4m3fn_x4
+ACT = mybir.ActivationFunctionType
+ALU = mybir.AluOpType
+
+P = 128
+PACK = 4
+K_PASS = P * PACK
+N_TILE = 512
+QUADRANTS = 4
+PLANES_PER_SLOT = 4
+
+GATES = 7
+D = 512
+H = 1024
+PASSES1 = (D + H) // K_PASS
+PASSES2 = H // K_PASS
+HALVES = H // N_TILE
+
+INPUT = 0
+FORGET = 1
+INPUT_TARGET = 2
+FORGET_TARGET = 3
+OUTPUT = 4
+Z = 5
+DECAY = 6
+GATE_ORDER = (DECAY, Z, FORGET_TARGET, INPUT_TARGET, FORGET, INPUT, OUTPUT)
+
+RESULT_TILES = 3 * HALVES
+
+FLOPS = 2 * P * (D + H + H) * H * GATES
+
+
+def columns(half):
+    return slice(half * N_TILE, (half + 1) * N_TILE)
+
+
+def word_bytes(half):
+    return slice(PACK * half * N_TILE, PACK * (half + 1) * N_TILE)
+
+
+def place_planes(n_groups):
+    slots = []
+    where = {}
+    for end in range(n_groups, 0, -PLANES_PER_SLOT):
+        first = max(end - PLANES_PER_SLOT, 0)
+        for group in range(first, end):
+            where[group] = (len(slots), 4 * (group - first))
+        slots.append((first, end))
+    return slots, where
+
+
+def tile_hawkeslstmcell_pa_e_kernel(
+    tc, x, h_t, c_t, c_target, W1_words, W1_scales, b1, W2_words, W2_scales, b2, out_0, out_1, out_2, out_3
+):
+    nc = tc.nc
+    with ExitStack() as ctx:
+        const = ctx.enter_context(tc.tile_pool(name="const", bufs=1))
+        work = ctx.enter_context(tc.tile_pool(name="work", bufs=2))
+        psum = ctx.enter_context(tc.psum_pool(name="psum", bufs=2))
+        ctx.enter_context(tc.manual_schedule())
+
+        w1_words = [const.tile([P, PASSES1, PACK * H], U8, name="w1_words%d" % e, align_bytes=64) for e in range(GATES)]
+        w2_words = [const.tile([P, PASSES2, PACK * H], U8, name="w2_words%d" % e, align_bytes=64) for e in range(GATES)]
+        w1_slots, w1_where = place_planes(GATES * PASSES1)
+        w2_slots, w2_where = place_planes(GATES * PASSES2)
+        w1_planes = [const.tile([P, H], U8, name="w1_planes%d" % s, align_bytes=64) for s in range(len(w1_slots))]
+        w2_planes = [const.tile([P, H], U8, name="w2_planes%d" % s, align_bytes=64) for s in range(len(w2_slots))]
+
+        v_sb = const.tile([P, D + H], BF16)
+        b1_rows = const.tile([P, N_TILE], BF16)
+        b2_rows = const.tile([P, H], BF16)
+        old_cell = {
+            FORGET: (c_t, const.tile([P, H], BF16, name="c_t_sb")),
+            FORGET_TARGET: (c_target, const.tile([P, H], BF16, name="c_target_sb")),
+        }
+
+        nc.vector.memset(b1_rows[:], 0.0)
+        for plane in w1_planes:
+            nc.vector.memset(plane[:].bitcast(I32), 0)
+        nc.vector.memset(b2_rows[:], 0.0)
+        for plane in w2_planes:
+            nc.vector.memset(plane[:].bitcast(I32), 0)
+
+        loaded = set()
+
+        def load_scales(key, planes, slots, where, scales, groups):
+            for group in groups:
+                s = where[group][0]
+                if (key, s) in loaded:
+                    continue
+                loaded.add((key, s))
+                first, end = slots[s]
+                for quadrant in range(QUADRANTS):
+                    nc.sync.dma_start(
+                        out=planes[s][32 * quadrant : 32 * quadrant + 4 * (end - first), :].bitcast(I32),
+                        in_=scales[first:end, 4 * quadrant : 4 * quadrant + 4, :].bitcast(I32),
+                    )
+
+        def load_w1(e):
+            groups = range(PASSES1 * e, PASSES1 * (e + 1))
+            load_scales("w1", w1_planes, w1_slots, w1_where, W1_scales, groups)
+            nc.sync.dma_start(
+                out=w1_words[e][:].bitcast(I32),
+                in_=W1_words[PASSES1 * e : PASSES1 * (e + 1)].rearrange("g p n t -> p g (n t)").bitcast(I32),
+            )
+
+        def load_w2(e):
+            groups = range(PASSES2 * e, PASSES2 * (e + 1))
+            load_scales("w2", w2_planes, w2_slots, w2_where, W2_scales, groups)
+            if e in old_cell:
+                nc.sync.dma_start(out=old_cell[e][1][:], in_=old_cell[e][0])
+            nc.sync.dma_start(
+                out=w2_words[e][:].bitcast(I32),
+                in_=W2_words[PASSES2 * e : PASSES2 * (e + 1)].rearrange("g p n t -> p g (n t)").bitcast(I32),
+            )
+
+        nc.sync.dma_start(out=v_sb[:, 0:D], in_=x)
+        nc.sync.dma_start(out=v_sb[:, D : D + H], in_=h_t)
+        nc.sync.dma_start(out=b1_rows[0 : GATES * HALVES, :], in_=b1.rearrange("e (g n) -> (e g) n", g=HALVES))
+        load_w1(GATE_ORDER[0])
+        nc.sync.dma_start(out=b2_rows[0:GATES, :], in_=b2)
+        load_w1(GATE_ORDER[1])
+        for i in range(GATES):
+            load_w2(GATE_ORDER[i])
+            if i + 2 < GATES:
+                load_w1(GATE_ORDER[i + 2])
+
+        ident_f32 = const.tile([P, P], F32)
+        ident_bf16 = const.tile([P, P], BF16)
+        make_identity(nc, ident_f32[:])
+        make_identity(nc, ident_bf16[:])
+
+        first_table = const.tile([P, 1], F32)
+        nc.gpsimd.memset(first_table[:], 0.0)
+        nc.scalar.activation(out=first_table[:], in_=first_table[:], func=ACT.Sigmoid)
+
+        v_pairs = v_sb[:].bitcast(F32)
+        v_grouped = const.tile([P, PASSES1, K_PASS], BF16, align_bytes=64)
+        v_codes = const.tile([P, PASSES1, P], U32, align_bytes=64)
+        v_scales = const.tile([P, PASSES1, P], U8, align_bytes=64)
+        for c in range(PASSES1):
+            v_flipped = psum.tile([P, 2, P], F32, tag="flipped")
+            for u in range(2):
+                nc.tensor.transpose(v_flipped[:, u, :], v_pairs[:, 256 * c + u : 256 * (c + 1) : 2], ident_f32[:])
+            nc.vector.tensor_copy(
+                out=v_grouped[:, c, :].bitcast(F32).rearrange("p (r u) -> p r u", u=2),
+                in_=v_flipped[:].rearrange("p u r -> p r u"),
+            )
+        for c in range(PASSES1):
+            nc.vector.quantize_mx(
+                out=v_codes[:, c, :].bitcast(FP8X4), scales=v_scales[:, c, :], in_=v_grouped[:, c, :]
+            )
+
+        b1_sorted = const.tile([P, PACK, P], BF16)
+        nc.vector.tensor_copy(out=b1_sorted[:], in_=b1_rows[:].rearrange("p (q t) -> p t q", t=PACK))
+        b1_ps = psum.tile([P, PACK, P], BF16, tag="bias_ps", bufs=1)
+        for t in range(PACK):
+            nc.tensor.transpose(b1_ps[:, t, :], b1_sorted[:, t, :], ident_bf16[:])
+        b1_t = const.tile([P, GATES * HALVES, PACK], F32)
+        nc.vector.tensor_copy(out=b1_t[:], in_=b1_ps[:, :, 0 : GATES * HALVES].rearrange("p t i -> p i t"))
+
+        def first_layer_products(e):
+            sorted_halves = []
+            for half in range(HALVES):
+                acc1 = psum.tile([P, N_TILE], F32, tag="acc1")
+                for c in range(PASSES1):
+                    s, k = w1_where[PASSES1 * e + c]
+                    nc.tensor.matmul_mx(
+                        out=acc1[:],
+                        lhsT=v_codes[:, c, :].bitcast(FP8X4),
+                        lhsT_scale=v_scales[:, c, :],
+                        rhs=w1_words[e][:, c, word_bytes(half)].bitcast(FP8X4),
+                        rhs_scale=w1_planes[s][k:P, columns(half)],
+                        start=(c == 0),
+                        stop=(c == PASSES1 - 1),
+                    )
+                h_sorted = work.tile([P, PACK, P], F32, tag="h_sorted", bufs=2 * HALVES)
+                nc.scalar.copy(out=h_sorted[:], in_=acc1[:].rearrange("p (q t) -> p t q", t=PACK))
+                sorted_halves.append(h_sorted)
+            return sorted_halves
+
+        def first_layer_squash(e, sorted_halves):
+            h_grouped = work.tile([P, PASSES2, K_PASS], BF16, tag="h_grouped", align_bytes=64)
+            for half in range(HALVES):
+                h_flipped = psum.tile([P, PACK, P], F32, tag="flipped")
+                for t in range(PACK):
+                    nc.tensor.transpose(h_flipped[:, t, :], sorted_halves[half][:, t, :], ident_f32[:])
+                h_pre = work.tile([P, P, PACK], F32, tag="h_pre")
+                nc.vector.tensor_tensor(
+                    out=h_pre[:],
+                    in0=h_flipped[:].rearrange("p t r -> p r t"),
+                    in1=b1_t[:, HALVES * e + half, :].unsqueeze(1).to_broadcast([P, P, PACK]),
+                    op=ALU.add,
+                )
+                nc.scalar.activation(
+                    out=h_grouped[:, half, :], in_=h_pre[:].rearrange("p r t -> p (r t)"), func=ACT.Tanh
+                )
+            return h_grouped
+
+        def first_layer_quantise(h_grouped):
+            h_codes = work.tile([P, PASSES2, P], U32, tag="h_codes", align_bytes=64)
+            h_scales = work.tile([P, PASSES2, P], U8, tag="h_scales", align_bytes=64)
+            nc.vector.quantize_mx(
+                out=h_codes[:].rearrange("p c r -> p (c r)").bitcast(FP8X4),
+                scales=h_scales[:].rearrange("p c r -> p (c r)"),
+                in_=h_grouped[:].rearrange("p c k -> p (c k)"),
+            )
+            return h_codes, h_scales
+
+        def spread_b2(e):
+            bias_ps = psum.tile([P, H], BF16, tag="bias_ps", bufs=1)
+            for half in range(HALVES):
+                nc.tensor.matmul(
+                    out=bias_ps[:, columns(half)],
+                    lhsT=ident_bf16[:, e : e + 1].to_broadcast([P, P]),
+                    rhs=b2_rows[:, columns(half)],
+                    start=True,
+                    stop=True,
+                )
+            b2_all = work.tile([P, H], BF16, tag="b2_all")
+            nc.scalar.copy(out=b2_all[:], in_=bias_ps[:])
+            return b2_all
+
+        z = const.tile([P, H], F32)
+        log_term = const.tile([P, H], F32)
+
+        def second_layer(e, h_codes, h_scales, b2_all):
+            halves = []
+            for half in range(HALVES):
+                acc2 = psum.tile([P, N_TILE], F32, tag="acc2")
+                for c in range(PASSES2):
+                    s, k = w2_where[PASSES2 * e + c]
+                    nc.tensor.matmul_mx(
+                        out=acc2[:],
+                        lhsT=h_codes[:, c, :].bitcast(FP8X4),
+                        lhsT_scale=h_scales[:, c, :],
+                        rhs=w2_words[e][:, c, word_bytes(half)].bitcast(FP8X4),
+                        rhs_scale=w2_planes[s][k:P, columns(half)],
+                        start=(c == 0),
+                        stop=(c == PASSES2 - 1),
+                    )
+                g = work.tile([P, N_TILE], F32, tag="g", bufs=2 * HALVES)
+                nc.vector.tensor_tensor(out=g[:], in0=acc2[:], in1=b2_all[:, columns(half)], op=ALU.add)
+                if e == DECAY:
+                    size = work.tile([P, N_TILE], F32, tag="value", bufs=2 * HALVES)
+                    nc.vector.scalar_tensor_tensor(
+                        out=size[:], in0=g[:], scalar=-1.0, in1=g[:], op0=ALU.mult, op1=ALU.max
+                    )
+                    value = log_term[:, columns(half)]
+                    nc.scalar.activation(out=value, in_=size[:], func=ACT.Sigmoid)
+                elif e == Z:
+                    value = z[:, columns(half)]
+                    nc.scalar.activation(out=value, in_=g[:], func=ACT.Tanh)
+                elif e == OUTPUT:
+                    result = work.tile([P, N_TILE], F32, tag="result", bufs=RESULT_TILES)
+                    value = result[:]
+                    nc.scalar.activation(out=value, in_=g[:], func=ACT.Sigmoid)
+                else:
+                    gate = work.tile([P, N_TILE], F32, tag="value", bufs=2 * HALVES)
+                    value = gate[:]
+                    nc.scalar.activation(out=value, in_=g[:], func=ACT.Sigmoid)
+                halves.append((g, value))
+            if e == DECAY:
+                nc.scalar.activation(out=log_term[:], in_=log_term[:], func=ACT.Ln)
+            return halves
+
+        kept = {}
+        new_cell = {INPUT: (out_0, FORGET), INPUT_TARGET: (out_1, FORGET_TARGET)}
+
+        def store(out, half, result):
+            nc.sync.dma_start(out=out[:, columns(half)], in_=result)
+
+        def finish(e, halves):
+            for half in range(HALVES):
+                g, value = halves[half]
+                if e == DECAY:
+                    nc.vector.scalar_tensor_tensor(
+                        out=value, in0=g[:], scalar=0.0, in1=value, op0=ALU.max, op1=ALU.subtract
+                    )
+                    store(out_3, half, value)
+                elif e == OUTPUT:
+                    store(out_2, half, value)
+                elif e in old_cell:
+                    kept_part = work.tile([P, N_TILE], F32, tag="kept_part")
+                    nc.vector.tensor_tensor(
+                        out=kept_part[:], in0=value, in1=old_cell[e][1][:, columns(half)], op=ALU.mult
+                    )
+                    kept[(e, half)] = kept_part
+                elif e in new_cell:
+                    out, forget = new_cell[e]
+                    nc.vector.tensor_tensor(out=value, in0=value, in1=z[:, columns(half)], op=ALU.mult)
+                    result = work.tile([P, N_TILE], F32, tag="result", bufs=RESULT_TILES)
+                    nc.vector.tensor_tensor(out=result[:], in0=value, in1=kept[(forget, half)][:], op=ALU.add)
+                    store(out, half, result[:])
+
+        sorted_halves = first_layer_products(GATE_ORDER[0])
+        h1 = first_layer_quantise(first_layer_squash(GATE_ORDER[0], sorted_halves))
+        sorted_halves = first_layer_products(GATE_ORDER[1])
+        b2_all = spread_b2(GATE_ORDER[0])
+        for i in range(GATES):
+            if i + 1 < GATES:
+                h_grouped = first_layer_squash(GATE_ORDER[i + 1], sorted_halves)
+            halves = second_layer(GATE_ORDER[i], h1[0], h1[1], b2_all)
+            if i + 1 < GATES:
+                h1 = first_layer_quantise(h_grouped)
+            finish(GATE_ORDER[i], halves)
+            if i + 2 < GATES:
+                sorted_halves = first_layer_products(GATE_ORDER[i + 2])
+            if i + 1 < GATES:
+                b2_all = spread_b2(GATE_ORDER[i + 1])

@@ -234,8 +234,8 @@ def tile_hawkeslstmcell_pa_e_kernel(
         z = const.tile([P, H], F32)
         log_term = const.tile([P, H], F32)
 
-        def second_layer(e, h_codes, h_scales, b2_all):
-            halves = []
+        def second_layer_products(e, h_codes, h_scales, b2_all):
+            g_halves = []
             for half in range(HALVES):
                 acc2 = psum.tile([P, N_TILE], F32, tag="acc2")
                 for c in range(PASSES2):
@@ -251,6 +251,13 @@ def tile_hawkeslstmcell_pa_e_kernel(
                     )
                 g = work.tile([P, N_TILE], F32, tag="g", bufs=2 * HALVES)
                 nc.vector.tensor_tensor(out=g[:], in0=acc2[:], in1=b2_all[:, columns(half)], op=ALU.add)
+                g_halves.append(g)
+            return g_halves
+
+        def gate_function(e, g_halves):
+            halves = []
+            for half in range(HALVES):
+                g = g_halves[half]
                 if e == DECAY:
                     size = work.tile([P, N_TILE], F32, tag="value", bufs=2 * HALVES)
                     nc.vector.scalar_tensor_tensor(
@@ -307,14 +314,19 @@ def tile_hawkeslstmcell_pa_e_kernel(
         h1 = first_layer_quantise(first_layer_squash(GATE_ORDER[0], sorted_halves))
         sorted_halves = first_layer_products(GATE_ORDER[1])
         b2_all = spread_b2(GATE_ORDER[0])
-        for i in range(GATES):
+        halves = {}
+        for i in range(GATES + 1):
             if i + 1 < GATES:
                 h_grouped = first_layer_squash(GATE_ORDER[i + 1], sorted_halves)
-            halves = second_layer(GATE_ORDER[i], h1[0], h1[1], b2_all)
+            if i < GATES:
+                g_halves = second_layer_products(GATE_ORDER[i], h1[0], h1[1], b2_all)
             if i + 1 < GATES:
                 h1 = first_layer_quantise(h_grouped)
-            finish(GATE_ORDER[i], halves)
+            if i >= 1:
+                finish(GATE_ORDER[i - 1], halves[i - 1])
             if i + 2 < GATES:
                 sorted_halves = first_layer_products(GATE_ORDER[i + 2])
+            if i < GATES:
+                halves[i] = gate_function(GATE_ORDER[i], g_halves)
             if i + 1 < GATES:
                 b2_all = spread_b2(GATE_ORDER[i + 1])

@@ -91,6 +91,15 @@ def tile_hawkeslstmcell_pa_e_kernel(
         for plane in w2_planes:
             nc.vector.memset(plane[:].bitcast(I32), 0)
 
+        ident_f32 = const.tile([P, P], F32)
+        ident_bf16 = const.tile([P, P], BF16)
+        make_identity(nc, ident_f32[:])
+        make_identity(nc, ident_bf16[:])
+
+        first_table = const.tile([P, 1], F32)
+        nc.gpsimd.memset(first_table[:], 0.0)
+        nc.scalar.activation(out=first_table[:], in_=first_table[:], func=ACT.Sigmoid)
+
         loaded = set()
 
         def load_scales(key, planes, slots, where, scales, groups):
@@ -98,12 +107,13 @@ def tile_hawkeslstmcell_pa_e_kernel(
                 s = where[group][0]
                 if (key, s) in loaded:
                     continue
+                queue, view = (nc.gpsimd, F32) if loaded else (nc.sync, I32)
                 loaded.add((key, s))
                 first, end = slots[s]
                 for quadrant in range(QUADRANTS):
-                    nc.sync.dma_start(
-                        out=planes[s][32 * quadrant : 32 * quadrant + 4 * (end - first), :].bitcast(I32),
-                        in_=scales[first:end, 4 * quadrant : 4 * quadrant + 4, :].bitcast(I32),
+                    queue.dma_start(
+                        out=planes[s][32 * quadrant : 32 * quadrant + 4 * (end - first), :].bitcast(view),
+                        in_=scales[first:end, 4 * quadrant : 4 * quadrant + 4, :].bitcast(view),
                     )
 
         def load_w1(e):
@@ -134,15 +144,6 @@ def tile_hawkeslstmcell_pa_e_kernel(
             load_w2(GATE_ORDER[i])
             if i + 2 < GATES:
                 load_w1(GATE_ORDER[i + 2])
-
-        ident_f32 = const.tile([P, P], F32)
-        ident_bf16 = const.tile([P, P], BF16)
-        make_identity(nc, ident_f32[:])
-        make_identity(nc, ident_bf16[:])
-
-        first_table = const.tile([P, 1], F32)
-        nc.gpsimd.memset(first_table[:], 0.0)
-        nc.scalar.activation(out=first_table[:], in_=first_table[:], func=ACT.Sigmoid)
 
         v_pairs = v_sb[:].bitcast(F32)
         v_grouped = const.tile([P, PASSES1, K_PASS], BF16, align_bytes=64)
@@ -234,8 +235,8 @@ def tile_hawkeslstmcell_pa_e_kernel(
         z = const.tile([P, H], F32)
         log_term = const.tile([P, H], F32)
 
-        def second_layer_products(e, h_codes, h_scales, b2_all):
-            g_halves = []
+        def second_layer(e, h_codes, h_scales, b2_all):
+            halves = []
             for half in range(HALVES):
                 acc2 = psum.tile([P, N_TILE], F32, tag="acc2")
                 for c in range(PASSES2):
@@ -251,13 +252,6 @@ def tile_hawkeslstmcell_pa_e_kernel(
                     )
                 g = work.tile([P, N_TILE], F32, tag="g", bufs=2 * HALVES)
                 nc.vector.tensor_tensor(out=g[:], in0=acc2[:], in1=b2_all[:, columns(half)], op=ALU.add)
-                g_halves.append(g)
-            return g_halves
-
-        def gate_function(e, g_halves):
-            halves = []
-            for half in range(HALVES):
-                g = g_halves[half]
                 if e == DECAY:
                     size = work.tile([P, N_TILE], F32, tag="value", bufs=2 * HALVES)
                     nc.vector.scalar_tensor_tensor(
@@ -314,19 +308,14 @@ def tile_hawkeslstmcell_pa_e_kernel(
         h1 = first_layer_quantise(first_layer_squash(GATE_ORDER[0], sorted_halves))
         sorted_halves = first_layer_products(GATE_ORDER[1])
         b2_all = spread_b2(GATE_ORDER[0])
-        halves = {}
-        for i in range(GATES + 1):
+        for i in range(GATES):
             if i + 1 < GATES:
                 h_grouped = first_layer_squash(GATE_ORDER[i + 1], sorted_halves)
-            if i < GATES:
-                g_halves = second_layer_products(GATE_ORDER[i], h1[0], h1[1], b2_all)
+            halves = second_layer(GATE_ORDER[i], h1[0], h1[1], b2_all)
             if i + 1 < GATES:
                 h1 = first_layer_quantise(h_grouped)
-            if i >= 1:
-                finish(GATE_ORDER[i - 1], halves[i - 1])
+            finish(GATE_ORDER[i], halves)
             if i + 2 < GATES:
                 sorted_halves = first_layer_products(GATE_ORDER[i + 2])
-            if i < GATES:
-                halves[i] = gate_function(GATE_ORDER[i], g_halves)
             if i + 1 < GATES:
                 b2_all = spread_b2(GATE_ORDER[i + 1])

@@ -84,8 +84,9 @@ def tile_hawkeslstmcell_pa_e_kernel(
             FORGET_TARGET: (c_target, const.tile([P, H], BF16, name="c_target_sb")),
         }
 
+        nc.vector.memset(w1_planes[0][:].bitcast(I32), 0)
         nc.vector.memset(b1_rows[:], 0.0)
-        for plane in w1_planes:
+        for plane in w1_planes[1:]:
             nc.vector.memset(plane[:].bitcast(I32), 0)
         nc.vector.memset(b2_rows[:], 0.0)
         for plane in w2_planes:
@@ -118,11 +119,14 @@ def tile_hawkeslstmcell_pa_e_kernel(
 
         def load_w1(e):
             groups = range(PASSES1 * e, PASSES1 * (e + 1))
-            load_scales("w1", w1_planes, w1_slots, w1_where, W1_scales, groups)
+            if loaded:
+                load_scales("w1", w1_planes, w1_slots, w1_where, W1_scales, groups)
             nc.sync.dma_start(
                 out=w1_words[e][:].bitcast(I32),
                 in_=W1_words[PASSES1 * e : PASSES1 * (e + 1)].rearrange("g p n t -> p g (n t)").bitcast(I32),
             )
+            if not loaded:
+                load_scales("w1", w1_planes, w1_slots, w1_where, W1_scales, groups)
 
         def load_w2(e):
             groups = range(PASSES2 * e, PASSES2 * (e + 1))
@@ -136,8 +140,8 @@ def tile_hawkeslstmcell_pa_e_kernel(
 
         nc.sync.dma_start(out=v_sb[:, 0:D], in_=x)
         nc.sync.dma_start(out=v_sb[:, D : D + H], in_=h_t)
-        nc.sync.dma_start(out=b1_rows[0 : GATES * HALVES, :], in_=b1.rearrange("e (g n) -> (e g) n", g=HALVES))
         load_w1(GATE_ORDER[0])
+        nc.sync.dma_start(out=b1_rows[0 : GATES * HALVES, :], in_=b1.rearrange("e (g n) -> (e g) n", g=HALVES))
         nc.sync.dma_start(out=b2_rows[0:GATES, :], in_=b2)
         load_w1(GATE_ORDER[1])
         for i in range(GATES):
@@ -161,14 +165,6 @@ def tile_hawkeslstmcell_pa_e_kernel(
             nc.vector.quantize_mx(
                 out=v_codes[:, c, :].bitcast(FP8X4), scales=v_scales[:, c, :], in_=v_grouped[:, c, :]
             )
-
-        b1_sorted = const.tile([P, PACK, P], BF16)
-        nc.vector.tensor_copy(out=b1_sorted[:], in_=b1_rows[:].rearrange("p (q t) -> p t q", t=PACK))
-        b1_ps = psum.tile([P, PACK, P], BF16, tag="bias_ps", bufs=1)
-        for t in range(PACK):
-            nc.tensor.transpose(b1_ps[:, t, :], b1_sorted[:, t, :], ident_bf16[:])
-        b1_t = const.tile([P, GATES * HALVES, PACK], F32)
-        nc.vector.tensor_copy(out=b1_t[:], in_=b1_ps[:, :, 0 : GATES * HALVES].rearrange("p t i -> p i t"))
 
         def first_layer_products(e):
             sorted_halves = []
@@ -305,6 +301,15 @@ def tile_hawkeslstmcell_pa_e_kernel(
                     store(out, half, result[:])
 
         sorted_halves = first_layer_products(GATE_ORDER[0])
+
+        b1_sorted = const.tile([P, PACK, P], BF16)
+        nc.vector.tensor_copy(out=b1_sorted[:], in_=b1_rows[:].rearrange("p (q t) -> p t q", t=PACK))
+        b1_ps = psum.tile([P, PACK, P], BF16, tag="bias_ps", bufs=1)
+        for t in range(PACK):
+            nc.tensor.transpose(b1_ps[:, t, :], b1_sorted[:, t, :], ident_bf16[:])
+        b1_t = const.tile([P, GATES * HALVES, PACK], F32)
+        nc.vector.tensor_copy(out=b1_t[:], in_=b1_ps[:, :, 0 : GATES * HALVES].rearrange("p t i -> p i t"))
+
         h1 = first_layer_quantise(first_layer_squash(GATE_ORDER[0], sorted_halves))
         sorted_halves = first_layer_products(GATE_ORDER[1])
         b2_all = spread_b2(GATE_ORDER[0])

@@ -36,8 +36,13 @@ DECAY = 6
 GATE_ORDER = (DECAY, Z, FORGET_TARGET, INPUT_TARGET, FORGET, INPUT, OUTPUT)
 
 RESULT_TILES = 3 * HALVES
+SHORT_TILES = 2 * HALVES
 
 FLOPS = 2 * P * (D + H + H) * H * GATES
+
+LEAD = 2
+SCALES_ON_GPSIMD = True
+CELLS_ON_GPSIMD = False
 
 
 def columns(half):
@@ -86,10 +91,8 @@ def tile_hawkeslstmcell_pa_e_kernel(
 
         nc.vector.memset(w1_planes[0][:].bitcast(I32), 0)
         nc.vector.memset(b1_rows[:], 0.0)
-        for plane in w1_planes[1:]:
-            nc.vector.memset(plane[:].bitcast(I32), 0)
         nc.vector.memset(b2_rows[:], 0.0)
-        for plane in w2_planes:
+        for plane in w1_planes[1:] + w2_planes:
             nc.vector.memset(plane[:].bitcast(I32), 0)
 
         ident_f32 = const.tile([P, P], F32)
@@ -108,7 +111,7 @@ def tile_hawkeslstmcell_pa_e_kernel(
                 s = where[group][0]
                 if (key, s) in loaded:
                     continue
-                queue, view = (nc.gpsimd, F32) if loaded else (nc.sync, I32)
+                queue, view = (nc.gpsimd, F32) if (loaded and SCALES_ON_GPSIMD) else (nc.sync, I32)
                 loaded.add((key, s))
                 first, end = slots[s]
                 for quadrant in range(QUADRANTS):
@@ -143,11 +146,12 @@ def tile_hawkeslstmcell_pa_e_kernel(
         load_w1(GATE_ORDER[0])
         nc.sync.dma_start(out=b1_rows[0 : GATES * HALVES, :], in_=b1.rearrange("e (g n) -> (e g) n", g=HALVES))
         nc.sync.dma_start(out=b2_rows[0:GATES, :], in_=b2)
-        load_w1(GATE_ORDER[1])
+        for j in range(1, LEAD + 1):
+            load_w1(GATE_ORDER[j])
         for i in range(GATES):
             load_w2(GATE_ORDER[i])
-            if i + 2 < GATES:
-                load_w1(GATE_ORDER[i + 2])
+            if i + LEAD + 1 < GATES:
+                load_w1(GATE_ORDER[i + LEAD + 1])
 
         v_pairs = v_sb[:].bitcast(F32)
         v_grouped = const.tile([P, PASSES1, K_PASS], BF16, align_bytes=64)
@@ -165,6 +169,31 @@ def tile_hawkeslstmcell_pa_e_kernel(
             nc.vector.quantize_mx(
                 out=v_codes[:, c, :].bitcast(FP8X4), scales=v_scales[:, c, :], in_=v_grouped[:, c, :]
             )
+
+        b1_sorted = const.tile([P, PACK, P], BF16)
+        b1_t = const.tile([P, GATES * HALVES, PACK], F32)
+
+        def turn_b1():
+            nc.vector.tensor_copy(out=b1_sorted[:], in_=b1_rows[:].rearrange("p (q t) -> p t q", t=PACK))
+            b1_ps = psum.tile([P, PACK, P], BF16, tag="bias_ps")
+            for t in range(PACK):
+                nc.tensor.transpose(b1_ps[:, t, :], b1_sorted[:, t, :], ident_bf16[:])
+            nc.vector.tensor_copy(out=b1_t[:], in_=b1_ps[:, :, 0 : GATES * HALVES].rearrange("p t i -> p i t"))
+
+        b2_all = const.tile([P, GATES, H], BF16)
+
+        def spread_b2(i):
+            e = GATE_ORDER[i]
+            bias_ps = psum.tile([P, H], BF16, tag="bias_ps")
+            for half in range(HALVES):
+                nc.tensor.matmul(
+                    out=bias_ps[:, columns(half)],
+                    lhsT=ident_bf16[:, e : e + 1].to_broadcast([P, P]),
+                    rhs=b2_rows[:, columns(half)],
+                    start=True,
+                    stop=True,
+                )
+            nc.scalar.copy(out=b2_all[:, e, :], in_=bias_ps[:])
 
         def first_layer_products(e):
             sorted_halves = []
@@ -205,8 +234,8 @@ def tile_hawkeslstmcell_pa_e_kernel(
             return h_grouped
 
         def first_layer_quantise(h_grouped):
-            h_codes = work.tile([P, PASSES2, P], U32, tag="h_codes", align_bytes=64)
-            h_scales = work.tile([P, PASSES2, P], U8, tag="h_scales", align_bytes=64)
+            h_codes = work.tile([P, PASSES2, P], U32, tag="h_codes", align_bytes=64, bufs=LEAD + 1)
+            h_scales = work.tile([P, PASSES2, P], U8, tag="h_scales", align_bytes=64, bufs=LEAD + 1)
             nc.vector.quantize_mx(
                 out=h_codes[:].rearrange("p c r -> p (c r)").bitcast(FP8X4),
                 scales=h_scales[:].rearrange("p c r -> p (c r)"),
@@ -214,24 +243,13 @@ def tile_hawkeslstmcell_pa_e_kernel(
             )
             return h_codes, h_scales
 
-        def spread_b2(e):
-            bias_ps = psum.tile([P, H], BF16, tag="bias_ps", bufs=1)
-            for half in range(HALVES):
-                nc.tensor.matmul(
-                    out=bias_ps[:, columns(half)],
-                    lhsT=ident_bf16[:, e : e + 1].to_broadcast([P, P]),
-                    rhs=b2_rows[:, columns(half)],
-                    start=True,
-                    stop=True,
-                )
-            b2_all = work.tile([P, H], BF16, tag="b2_all")
-            nc.scalar.copy(out=b2_all[:], in_=bias_ps[:])
-            return b2_all
-
         z = const.tile([P, H], F32)
         log_term = const.tile([P, H], F32)
+        new_cell = {INPUT: (out_0, FORGET), INPUT_TARGET: (out_1, FORGET_TARGET)}
+        stored = (INPUT, INPUT_TARGET, OUTPUT)
 
-        def second_layer(e, h_codes, h_scales, b2_all):
+
+        def second_layer(e, h_codes, h_scales):
             halves = []
             for half in range(HALVES):
                 acc2 = psum.tile([P, N_TILE], F32, tag="acc2")
@@ -246,81 +264,73 @@ def tile_hawkeslstmcell_pa_e_kernel(
                         start=(c == 0),
                         stop=(c == PASSES2 - 1),
                     )
-                g = work.tile([P, N_TILE], F32, tag="g", bufs=2 * HALVES)
-                nc.vector.tensor_tensor(out=g[:], in0=acc2[:], in1=b2_all[:, columns(half)], op=ALU.add)
-                if e == DECAY:
-                    size = work.tile([P, N_TILE], F32, tag="value", bufs=2 * HALVES)
-                    nc.vector.scalar_tensor_tensor(
-                        out=size[:], in0=g[:], scalar=-1.0, in1=g[:], op0=ALU.mult, op1=ALU.max
-                    )
-                    value = log_term[:, columns(half)]
-                    nc.scalar.activation(out=value, in_=size[:], func=ACT.Sigmoid)
-                elif e == Z:
-                    value = z[:, columns(half)]
-                    nc.scalar.activation(out=value, in_=g[:], func=ACT.Tanh)
-                elif e == OUTPUT:
+                if e == Z:
+                    g = z[:, columns(half)]
+                elif e in stored:
                     result = work.tile([P, N_TILE], F32, tag="result", bufs=RESULT_TILES)
-                    value = result[:]
-                    nc.scalar.activation(out=value, in_=g[:], func=ACT.Sigmoid)
+                    g = result[:]
                 else:
-                    gate = work.tile([P, N_TILE], F32, tag="value", bufs=2 * HALVES)
-                    value = gate[:]
-                    nc.scalar.activation(out=value, in_=g[:], func=ACT.Sigmoid)
-                halves.append((g, value))
+                    short = work.tile([P, N_TILE], F32, tag="short", bufs=SHORT_TILES)
+                    g = short[:]
+                nc.vector.tensor_tensor(out=g, in0=acc2[:], in1=b2_all[:, e, columns(half)], op=ALU.add)
+                if e == DECAY:
+                    size = work.tile([P, N_TILE], F32, tag="short", bufs=SHORT_TILES)
+                    nc.vector.scalar_tensor_tensor(out=size[:], in0=g, scalar=-1.0, in1=g, op0=ALU.mult, op1=ALU.max)
+                    nc.scalar.activation(out=log_term[:, columns(half)], in_=size[:], func=ACT.Sigmoid)
+                elif e == Z:
+                    nc.scalar.activation(out=g, in_=g, func=ACT.Tanh)
+                else:
+                    nc.scalar.activation(out=g, in_=g, func=ACT.Sigmoid)
+                halves.append(g)
             if e == DECAY:
                 nc.scalar.activation(out=log_term[:], in_=log_term[:], func=ACT.Ln)
             return halves
 
         kept = {}
-        new_cell = {INPUT: (out_0, FORGET), INPUT_TARGET: (out_1, FORGET_TARGET)}
+        cells = nc.gpsimd if CELLS_ON_GPSIMD else nc.vector
 
         def store(out, half, result):
             nc.sync.dma_start(out=out[:, columns(half)], in_=result)
 
-        def finish(e, halves):
-            for half in range(HALVES):
-                g, value = halves[half]
+        def finish(e, halves, which):
+            for half in which:
+                g = halves[half]
                 if e == DECAY:
-                    nc.vector.scalar_tensor_tensor(
-                        out=value, in0=g[:], scalar=0.0, in1=value, op0=ALU.max, op1=ALU.subtract
-                    )
+                    value = log_term[:, columns(half)]
+                    nc.vector.scalar_tensor_tensor(out=value, in0=g, scalar=0.0, in1=value, op0=ALU.max, op1=ALU.subtract)
                     store(out_3, half, value)
                 elif e == OUTPUT:
-                    store(out_2, half, value)
+                    store(out_2, half, g)
                 elif e in old_cell:
-                    kept_part = work.tile([P, N_TILE], F32, tag="kept_part")
-                    nc.vector.tensor_tensor(
-                        out=kept_part[:], in0=value, in1=old_cell[e][1][:, columns(half)], op=ALU.mult
-                    )
-                    kept[(e, half)] = kept_part
+                    cells.tensor_tensor(out=g, in0=g, in1=old_cell[e][1][:, columns(half)], op=ALU.mult)
+                    kept[(e, half)] = g
                 elif e in new_cell:
                     out, forget = new_cell[e]
-                    nc.vector.tensor_tensor(out=value, in0=value, in1=z[:, columns(half)], op=ALU.mult)
-                    result = work.tile([P, N_TILE], F32, tag="result", bufs=RESULT_TILES)
-                    nc.vector.tensor_tensor(out=result[:], in0=value, in1=kept[(forget, half)][:], op=ALU.add)
-                    store(out, half, result[:])
+                    cells.tensor_tensor(out=g, in0=g, in1=z[:, columns(half)], op=ALU.mult)
+                    cells.tensor_tensor(out=g, in0=g, in1=kept[(forget, half)], op=ALU.add)
+                    store(out, half, g)
 
-        sorted_halves = first_layer_products(GATE_ORDER[0])
-
-        b1_sorted = const.tile([P, PACK, P], BF16)
-        nc.vector.tensor_copy(out=b1_sorted[:], in_=b1_rows[:].rearrange("p (q t) -> p t q", t=PACK))
-        b1_ps = psum.tile([P, PACK, P], BF16, tag="bias_ps", bufs=1)
-        for t in range(PACK):
-            nc.tensor.transpose(b1_ps[:, t, :], b1_sorted[:, t, :], ident_bf16[:])
-        b1_t = const.tile([P, GATES * HALVES, PACK], F32)
-        nc.vector.tensor_copy(out=b1_t[:], in_=b1_ps[:, :, 0 : GATES * HALVES].rearrange("p t i -> p i t"))
-
-        h1 = first_layer_quantise(first_layer_squash(GATE_ORDER[0], sorted_halves))
-        sorted_halves = first_layer_products(GATE_ORDER[1])
-        b2_all = spread_b2(GATE_ORDER[0])
-        for i in range(GATES):
-            if i + 1 < GATES:
-                h_grouped = first_layer_squash(GATE_ORDER[i + 1], sorted_halves)
-            halves = second_layer(GATE_ORDER[i], h1[0], h1[1], b2_all)
-            if i + 1 < GATES:
-                h1 = first_layer_quantise(h_grouped)
-            finish(GATE_ORDER[i], halves)
-            if i + 2 < GATES:
-                sorted_halves = first_layer_products(GATE_ORDER[i + 2])
-            if i + 1 < GATES:
-                b2_all = spread_b2(GATE_ORDER[i + 1])
+        sorted_halves = {}
+        h1 = {}
+        every = tuple(range(HALVES))
+        for t in range(-LEAD - 1, GATES):
+            j = t + LEAD
+            if 0 <= j < GATES:
+                h_grouped = first_layer_squash(GATE_ORDER[j], sorted_halves[j])
+            if t >= 0:
+                halves = second_layer(GATE_ORDER[t], h1[t][0], h1[t][1])
+            if 0 <= j < GATES:
+                h1[j] = first_layer_quantise(h_grouped)
+            if t == GATES - 1:
+                finish(GATE_ORDER[t], halves, every)
+                finish(GATE_ORDER[t - 1], before, every[1:])
+            elif t == GATES - 2:
+                finish(GATE_ORDER[t], halves, every[:1])
+                before = halves
+            elif t >= 0:
+                finish(GATE_ORDER[t], halves, every)
+            if j + 1 < GATES:
+                sorted_halves[j + 1] = first_layer_products(GATE_ORDER[j + 1])
+                if j + 1 == 0:
+                    turn_b1()
+                spread_b2(j + 1)

from contextlib import ExitStack

import concourse.mybir as mybir
from concourse.masks import make_identity

F32 = mybir.dt.float32
BF16 = mybir.dt.bfloat16
I32 = mybir.dt.int32
U32 = mybir.dt.uint32
U8 = mybir.dt.uint8
FP8X4 = mybir.dt.float8_e4m3fn_x4
ACT = mybir.ActivationFunctionType
ALU = mybir.AluOpType

P = 128
PACK = 4
K_PASS = P * PACK
N_TILE = 512
QUADRANTS = 4
PLANES_PER_SLOT = 4

GATES = 7
D = 512
H = 1024
PASSES1 = (D + H) // K_PASS
PASSES2 = H // K_PASS
HALVES = H // N_TILE

INPUT = 0
FORGET = 1
INPUT_TARGET = 2
FORGET_TARGET = 3
OUTPUT = 4
Z = 5
DECAY = 6
GATE_ORDER = (DECAY, Z, FORGET_TARGET, INPUT_TARGET, FORGET, INPUT, OUTPUT)

RESULT_TILES = 3 * HALVES
SHORT_TILES = 2 * HALVES

FLOPS = 2 * P * (D + H + H) * H * GATES

LEAD = 2
SCALES_ON_GPSIMD = True
CELLS_ON_GPSIMD = False


def columns(half):
    return slice(half * N_TILE, (half + 1) * N_TILE)


def word_bytes(half):
    return slice(PACK * half * N_TILE, PACK * (half + 1) * N_TILE)


def place_planes(n_groups):
    slots = []
    where = {}
    for end in range(n_groups, 0, -PLANES_PER_SLOT):
        first = max(end - PLANES_PER_SLOT, 0)
        for group in range(first, end):
            where[group] = (len(slots), 4 * (group - first))
        slots.append((first, end))
    return slots, where


def tile_hawkeslstmcell_pa_e_kernel(
    tc, x, h_t, c_t, c_target, W1_words, W1_scales, b1, W2_words, W2_scales, b2, out_0, out_1, out_2, out_3
):
    nc = tc.nc
    with ExitStack() as ctx:
        const = ctx.enter_context(tc.tile_pool(name="const", bufs=1))
        work = ctx.enter_context(tc.tile_pool(name="work", bufs=2))
        psum = ctx.enter_context(tc.psum_pool(name="psum", bufs=2))
        ctx.enter_context(tc.manual_schedule())

        w1_words = [const.tile([P, PASSES1, PACK * H], U8, name="w1_words%d" % e, align_bytes=64) for e in range(GATES)]
        w2_words = [const.tile([P, PASSES2, PACK * H], U8, name="w2_words%d" % e, align_bytes=64) for e in range(GATES)]
        w1_slots, w1_where = place_planes(GATES * PASSES1)
        w2_slots, w2_where = place_planes(GATES * PASSES2)
        w1_planes = [const.tile([P, H], U8, name="w1_planes%d" % s, align_bytes=64) for s in range(len(w1_slots))]
        w2_planes = [const.tile([P, H], U8, name="w2_planes%d" % s, align_bytes=64) for s in range(len(w2_slots))]

        v_sb = const.tile([P, D + H], BF16)
        b1_rows = const.tile([P, N_TILE], BF16)
        b2_rows = const.tile([P, H], BF16)
        old_cell = {
            FORGET: (c_t, const.tile([P, H], BF16, name="c_t_sb")),
            FORGET_TARGET: (c_target, const.tile([P, H], BF16, name="c_target_sb")),
        }

        nc.vector.memset(w1_planes[0][:].bitcast(I32), 0)
        nc.vector.memset(b1_rows[:], 0.0)
        nc.vector.memset(b2_rows[:], 0.0)
        for plane in w1_planes[1:] + w2_planes:
            nc.vector.memset(plane[:].bitcast(I32), 0)

        ident_f32 = const.tile([P, P], F32)
        ident_bf16 = const.tile([P, P], BF16)
        make_identity(nc, ident_f32[:])
        make_identity(nc, ident_bf16[:])

        first_table = const.tile([P, 1], F32)
        nc.gpsimd.memset(first_table[:], 0.0)
        nc.scalar.activation(out=first_table[:], in_=first_table[:], func=ACT.Sigmoid)

        loaded = set()

        def load_scales(key, planes, slots, where, scales, groups):
            for group in groups:
                s = where[group][0]
                if (key, s) in loaded:
                    continue
                queue, view = (nc.gpsimd, F32) if (loaded and SCALES_ON_GPSIMD) else (nc.sync, I32)
                loaded.add((key, s))
                first, end = slots[s]
                for quadrant in range(QUADRANTS):
                    queue.dma_start(
                        out=planes[s][32 * quadrant : 32 * quadrant + 4 * (end - first), :].bitcast(view),
                        in_=scales[first:end, 4 * quadrant : 4 * quadrant + 4, :].bitcast(view),
                    )

        def load_w1(e):
            groups = range(PASSES1 * e, PASSES1 * (e + 1))
            if loaded:
                load_scales("w1", w1_planes, w1_slots, w1_where, W1_scales, groups)
            nc.sync.dma_start(
                out=w1_words[e][:].bitcast(I32),
                in_=W1_words[PASSES1 * e : PASSES1 * (e + 1)].rearrange("g p n t -> p g (n t)").bitcast(I32),
            )
            if not loaded:
                load_scales("w1", w1_planes, w1_slots, w1_where, W1_scales, groups)

        def load_w2(e):
            groups = range(PASSES2 * e, PASSES2 * (e + 1))
            load_scales("w2", w2_planes, w2_slots, w2_where, W2_scales, groups)
            if e in old_cell:
                nc.sync.dma_start(out=old_cell[e][1][:], in_=old_cell[e][0])
            nc.sync.dma_start(
                out=w2_words[e][:].bitcast(I32),
                in_=W2_words[PASSES2 * e : PASSES2 * (e + 1)].rearrange("g p n t -> p g (n t)").bitcast(I32),
            )

        nc.sync.dma_start(out=v_sb[:, 0:D], in_=x)
        nc.sync.dma_start(out=v_sb[:, D : D + H], in_=h_t)
        load_w1(GATE_ORDER[0])
        nc.sync.dma_start(out=b1_rows[0 : GATES * HALVES, :], in_=b1.rearrange("e (g n) -> (e g) n", g=HALVES))
        nc.sync.dma_start(out=b2_rows[0:GATES, :], in_=b2)
        for j in range(1, LEAD + 1):
            load_w1(GATE_ORDER[j])
        for i in range(GATES):
            load_w2(GATE_ORDER[i])
            if i + LEAD + 1 < GATES:
                load_w1(GATE_ORDER[i + LEAD + 1])

        v_pairs = v_sb[:].bitcast(F32)
        v_grouped = const.tile([P, PASSES1, K_PASS], BF16, align_bytes=64)
        v_codes = const.tile([P, PASSES1, P], U32, align_bytes=64)
        v_scales = const.tile([P, PASSES1, P], U8, align_bytes=64)
        for c in range(PASSES1):
            v_flipped = psum.tile([P, 2, P], F32, tag="flipped")
            for u in range(2):
                nc.tensor.transpose(v_flipped[:, u, :], v_pairs[:, 256 * c + u : 256 * (c + 1) : 2], ident_f32[:])
            nc.vector.tensor_copy(
                out=v_grouped[:, c, :].bitcast(F32).rearrange("p (r u) -> p r u", u=2),
                in_=v_flipped[:].rearrange("p u r -> p r u"),
            )
        for c in range(PASSES1):
            nc.vector.quantize_mx(
                out=v_codes[:, c, :].bitcast(FP8X4), scales=v_scales[:, c, :], in_=v_grouped[:, c, :]
            )

        b1_sorted = const.tile([P, PACK, P], BF16)
        b1_t = const.tile([P, GATES * HALVES, PACK], F32)

        def turn_b1():
            nc.vector.tensor_copy(out=b1_sorted[:], in_=b1_rows[:].rearrange("p (q t) -> p t q", t=PACK))
            b1_ps = psum.tile([P, PACK, P], BF16, tag="bias_ps")
            for t in range(PACK):
                nc.tensor.transpose(b1_ps[:, t, :], b1_sorted[:, t, :], ident_bf16[:])
            nc.vector.tensor_copy(out=b1_t[:], in_=b1_ps[:, :, 0 : GATES * HALVES].rearrange("p t i -> p i t"))

        b2_all = const.tile([P, GATES, H], BF16)

        def spread_b2(i):
            e = GATE_ORDER[i]
            bias_ps = psum.tile([P, H], BF16, tag="bias_ps")
            for half in range(HALVES):
                nc.tensor.matmul(
                    out=bias_ps[:, columns(half)],
                    lhsT=ident_bf16[:, e : e + 1].to_broadcast([P, P]),
                    rhs=b2_rows[:, columns(half)],
                    start=True,
                    stop=True,
                )
            nc.scalar.copy(out=b2_all[:, e, :], in_=bias_ps[:])

        def first_layer_products(e):
            sorted_halves = []
            for half in range(HALVES):
                acc1 = psum.tile([P, N_TILE], F32, tag="acc1")
                for c in range(PASSES1):
                    s, k = w1_where[PASSES1 * e + c]
                    nc.tensor.matmul_mx(
                        out=acc1[:],
                        lhsT=v_codes[:, c, :].bitcast(FP8X4),
                        lhsT_scale=v_scales[:, c, :],
                        rhs=w1_words[e][:, c, word_bytes(half)].bitcast(FP8X4),
                        rhs_scale=w1_planes[s][k:P, columns(half)],
                        start=(c == 0),
                        stop=(c == PASSES1 - 1),
                    )
                h_sorted = work.tile([P, PACK, P], F32, tag="h_sorted", bufs=2 * HALVES)
                nc.scalar.copy(out=h_sorted[:], in_=acc1[:].rearrange("p (q t) -> p t q", t=PACK))
                sorted_halves.append(h_sorted)
            return sorted_halves

        def first_layer_squash(e, sorted_halves):
            h_grouped = work.tile([P, PASSES2, K_PASS], BF16, tag="h_grouped", align_bytes=64)
            for half in range(HALVES):
                h_flipped = psum.tile([P, PACK, P], F32, tag="flipped")
                for t in range(PACK):
                    nc.tensor.transpose(h_flipped[:, t, :], sorted_halves[half][:, t, :], ident_f32[:])
                h_pre = work.tile([P, P, PACK], F32, tag="h_pre")
                nc.vector.tensor_tensor(
                    out=h_pre[:],
                    in0=h_flipped[:].rearrange("p t r -> p r t"),
                    in1=b1_t[:, HALVES * e + half, :].unsqueeze(1).to_broadcast([P, P, PACK]),
                    op=ALU.add,
                )
                nc.scalar.activation(
                    out=h_grouped[:, half, :], in_=h_pre[:].rearrange("p r t -> p (r t)"), func=ACT.Tanh
                )
            return h_grouped

        def first_layer_quantise(h_grouped):
            h_codes = work.tile([P, PASSES2, P], U32, tag="h_codes", align_bytes=64, bufs=LEAD + 1)
            h_scales = work.tile([P, PASSES2, P], U8, tag="h_scales", align_bytes=64, bufs=LEAD + 1)
            nc.vector.quantize_mx(
                out=h_codes[:].rearrange("p c r -> p (c r)").bitcast(FP8X4),
                scales=h_scales[:].rearrange("p c r -> p (c r)"),
                in_=h_grouped[:].rearrange("p c k -> p (c k)"),
            )
            return h_codes, h_scales

        z = const.tile([P, H], F32)
        log_term = const.tile([P, H], F32)
        new_cell = {INPUT: (out_0, FORGET), INPUT_TARGET: (out_1, FORGET_TARGET)}
        stored = (INPUT, INPUT_TARGET, OUTPUT)


        def second_layer(e, h_codes, h_scales):
            halves = []
            for half in range(HALVES):
                acc2 = psum.tile([P, N_TILE], F32, tag="acc2")
                for c in range(PASSES2):
                    s, k = w2_where[PASSES2 * e + c]
                    nc.tensor.matmul_mx(
                        out=acc2[:],
                        lhsT=h_codes[:, c, :].bitcast(FP8X4),
                        lhsT_scale=h_scales[:, c, :],
                        rhs=w2_words[e][:, c, word_bytes(half)].bitcast(FP8X4),
                        rhs_scale=w2_planes[s][k:P, columns(half)],
                        start=(c == 0),
                        stop=(c == PASSES2 - 1),
                    )
                if e == Z:
                    g = z[:, columns(half)]
                elif e in stored:
                    result = work.tile([P, N_TILE], F32, tag="result", bufs=RESULT_TILES)
                    g = result[:]
                else:
                    short = work.tile([P, N_TILE], F32, tag="short", bufs=SHORT_TILES)
                    g = short[:]
                nc.vector.tensor_tensor(out=g, in0=acc2[:], in1=b2_all[:, e, columns(half)], op=ALU.add)
                if e == DECAY:
                    size = work.tile([P, N_TILE], F32, tag="short", bufs=SHORT_TILES)
                    nc.vector.scalar_tensor_tensor(out=size[:], in0=g, scalar=-1.0, in1=g, op0=ALU.mult, op1=ALU.max)
                    nc.scalar.activation(out=log_term[:, columns(half)], in_=size[:], func=ACT.Sigmoid)
                elif e == Z:
                    nc.scalar.activation(out=g, in_=g, func=ACT.Tanh)
                else:
                    nc.scalar.activation(out=g, in_=g, func=ACT.Sigmoid)
                halves.append(g)
            if e == DECAY:
                nc.scalar.activation(out=log_term[:], in_=log_term[:], func=ACT.Ln)
            return halves

        kept = {}
        cells = nc.gpsimd if CELLS_ON_GPSIMD else nc.vector

        def store(out, half, result):
            nc.sync.dma_start(out=out[:, columns(half)], in_=result)

        def finish(e, halves, which):
            for half in which:
                g = halves[half]
                if e == DECAY:
                    value = log_term[:, columns(half)]
                    nc.vector.scalar_tensor_tensor(out=value, in0=g, scalar=0.0, in1=value, op0=ALU.max, op1=ALU.subtract)
                    store(out_3, half, value)
                elif e == OUTPUT:
                    store(out_2, half, g)
                elif e in old_cell:
                    cells.tensor_tensor(out=g, in0=g, in1=old_cell[e][1][:, columns(half)], op=ALU.mult)
                    kept[(e, half)] = g
                elif e in new_cell:
                    out, forget = new_cell[e]
                    cells.tensor_tensor(out=g, in0=g, in1=z[:, columns(half)], op=ALU.mult)
                    cells.tensor_tensor(out=g, in0=g, in1=kept[(forget, half)], op=ALU.add)
                    store(out, half, g)

        sorted_halves = {}
        h1 = {}
        every = tuple(range(HALVES))
        for t in range(-LEAD - 1, GATES):
            j = t + LEAD
            if 0 <= j < GATES:
                h_grouped = first_layer_squash(GATE_ORDER[j], sorted_halves[j])
            if t >= 0:
                halves = second_layer(GATE_ORDER[t], h1[t][0], h1[t][1])
            if 0 <= j < GATES:
                h1[j] = first_layer_quantise(h_grouped)
            if t == GATES - 1:
                finish(GATE_ORDER[t], halves, every)
                finish(GATE_ORDER[t - 1], before, every[1:])
            elif t == GATES - 2:
                finish(GATE_ORDER[t], halves, every[:1])
                before = halves
            elif t >= 0:
                finish(GATE_ORDER[t], halves, every)
            if j + 1 < GATES:
                sorted_halves[j + 1] = first_layer_products(GATE_ORDER[j + 1])
                if j + 1 == 0:
                    turn_b1()
                spread_b2(j + 1)
